import numpy as np
import ml_dtypes


def mxq(x, axis, fmt="e4m3"):
    dtype, down = {"e4m3": (ml_dtypes.float8_e4m3fn, 7), "e5m2": (ml_dtypes.float8_e5m2, 14)}[fmt]
    v = np.moveaxis(np.asarray(x, np.float32).astype(ml_dtypes.bfloat16).astype(np.float64), axis, -1)
    blocks = v.reshape(v.shape[:-1] + (-1, 32))
    amax = np.abs(blocks).max(-1, keepdims=True)
    byte = np.maximum(np.where(amax > 0, np.frexp(amax)[1] - 1 + 127, 0) - down, 1)
    scale = np.exp2(byte - 127.0)
    codes = (blocks / scale).astype(np.float32).astype(dtype).astype(np.float64)
    return np.moveaxis((codes * scale).reshape(v.shape), -1, axis)


WIDE = False


def mx_kscale(k):
    if not WIDE:
        return np.ones(k)
    levels = np.array([10, -10, 5, -5, 0])
    a = np.random.permutation(np.resize(levels, k // 512 * 4)).reshape(k // 512, 4)
    idx = np.arange(k)
    return np.exp2(a[idx // 512, idx % 128 // 32])


BF16 = ml_dtypes.bfloat16


def bf(x):
    return np.asarray(x, np.float32).astype(BF16)


def f64(x):
    return np.asarray(x).astype(np.float64)


N, K, H, A = 128, 2, 256, 5
D = K * H
T = A * H


def sigmoid(v):
    return 1.0 / (1.0 + np.exp(-v))


def setup_inputs():
    s = mx_kscale(D)
    h_mail = np.random.standard_normal((N, K, H)) * s.reshape(K, H)
    c_mail = np.random.standard_normal((N, K, H))
    U_f_w = np.random.standard_normal((T, T)) / np.sqrt(D)
    U_f_w[:D] = U_f_w[:D] / s[:, None]
    U_f_b = np.random.standard_normal(T) * 0.5
    U_iou_w = np.random.standard_normal((3 * H, T)) / np.sqrt(D)
    U_iou_w[:, :D] = U_iou_w[:, :D] / s
    b_iou = np.random.standard_normal((1, 3 * H)) * 0.3
    return {"h_mail": bf(h_mail), "c_mail": bf(c_mail), "U_f_w": bf(U_f_w), "U_f_b": bf(U_f_b), "U_iou_w": bf(U_iou_w), "b_iou": bf(b_iou)}


def reference(h_mail, c_mail, U_f_w, U_f_b, U_iou_w, b_iou):
    n, k, h = h_mail.shape
    d = k * h
    hq = mxq(f64(h_mail).reshape(n, d), 1, "e4m3")
    f = sigmoid((hq @ mxq(f64(U_f_w)[:d, :d], 0, "e4m3")) + f64(U_f_b)[:d])
    c_red = np.sum(f.reshape(n, k, h) * f64(c_mail), axis=1)
    iou = (hq @ mxq(f64(U_iou_w)[:, :d], 1, "e4m3").T) + f64(b_iou)
    i, o, u = np.split(iou, 3, axis=1)
    c = sigmoid(i) * np.tanh(u) + c_red
    h_out = sigmoid(o) * np.tanh(c)
    return h_out, c

@@ -1,0 +1,167 @@
+from contextlib import ExitStack
+
+import concourse.mybir as mybir
+from concourse.masks import make_identity
+
+F32 = mybir.dt.float32
+BF16 = mybir.dt.bfloat16
+U32 = mybir.dt.uint32
+U8 = mybir.dt.uint8
+FP8X4 = mybir.dt.float8_e4m3fn_x4
+ACT = mybir.ActivationFunctionType
+
+P = 128
+PACK = 4
+K = P * PACK
+H = 256
+HALVES = H // P
+
+F0 = 0
+I0 = 4
+O0 = 6
+U0 = 8
+F_TILES = 4
+GATE_TILES = 10
+IOU_ORDER = (I0, U0, I0 + 1, U0 + 1, O0, O0 + 1)
+
+FLOPS = 2 * P * K * GATE_TILES * P
+BYTES = 2 * (2 * P * K + K * K + K + 3 * H * K + 3 * H) + 4 * 2 * P * H
+
+
+def transpose_words(nc, psum, rows, ident_f32):
+    words = rows.bitcast(F32)
+    wordsT = psum.tile([P, 2, P], F32, tag="wordsT", name="wordsT")
+    for u in range(2):
+        nc.tensor.transpose(wordsT[:, u, :], words[:, u * P : (u + 1) * P], ident_f32[:])
+    return wordsT
+
+
+def tile_treelstmcell_s_kernel(tc, h_mail, c_mail, U_f_w, U_f_b, U_iou_w, b_iou, out_0, out_1):
+    nc = tc.nc
+    with ExitStack() as ctx:
+        sb = ctx.enter_context(tc.tile_pool(name="sb", bufs=1))
+        ps_in = ctx.enter_context(tc.psum_pool(name="ps_in", bufs=2))
+        ps_gate = ctx.enter_context(tc.psum_pool(name="ps_gate", bufs=3))
+        ps_keep = ctx.enter_context(tc.psum_pool(name="ps_keep", bufs=1))
+
+        ident_f32 = sb.tile([P, P], F32)
+        make_identity(nc, ident_f32[:])
+        ident_bf16 = sb.tile([P, P], BF16)
+        make_identity(nc, ident_bf16[:])
+        warm_in = sb.tile([P, 1], F32)
+        warm_out = sb.tile([P, 1], F32)
+        nc.vector.memset(warm_in[:], 0.0)
+        nc.scalar.activation(out=warm_out[:], in_=warm_in[:], func=ACT.Sigmoid)
+
+        bias_rows = sb.tile([P, P], BF16)
+        nc.vector.memset(bias_rows[:], 0.0)
+        nc.scalar.dma_start(out=bias_rows[F0:I0, :], in_=U_f_b[0:K].rearrange("(a p) -> a p", p=P))
+        nc.scalar.dma_start(out=bias_rows[I0:GATE_TILES, :], in_=b_iou.rearrange("o (a p) -> (o a) p", p=P))
+
+        uf_rows = sb.tile([P, PACK, K], BF16)
+        for u in range(2):
+            nc.sync.dma_start(
+                out=uf_rows[:, 2 * u : 2 * u + 2, :],
+                in_=U_f_w[2 * P * u : 2 * P * (u + 1), 0:K].rearrange("(p e) c -> p e c", e=2),
+            )
+        c_rows = sb.tile([P, K], BF16)
+        nc.sync.dma_start(out=c_rows[:], in_=c_mail.rearrange("n k h -> n (k h)"))
+        h_rows = sb.tile([P, K], BF16)
+        nc.sync.dma_start(out=h_rows[:], in_=h_mail.rearrange("n k h -> n (k h)"))
+        ui_rows = sb.tile([P, GATE_TILES - I0, K], BF16)
+        for m in IOU_ORDER:
+            nc.sync.dma_start(out=ui_rows[:, m - I0, :], in_=U_iou_w[(m - I0) * P : (m - I0 + 1) * P, 0:K])
+
+        biasT = ps_in.tile([P, P], BF16, tag="wordsT")
+        nc.tensor.transpose(biasT[:], bias_rows[:], ident_bf16[:])
+        bias_col = sb.tile([P, GATE_TILES], F32)
+        nc.vector.tensor_copy(out=bias_col[:], in_=biasT[:, 0:GATE_TILES])
+
+        w_grouped = sb.tile([P, GATE_TILES, P * PACK], BF16, align_bytes=64)
+        w_codes = sb.tile([P, GATE_TILES, P], U32, align_bytes=64)
+        w_scales = sb.tile([P, GATE_TILES, P], U8, align_bytes=64)
+        h_grouped = sb.tile([P, P * PACK], BF16, align_bytes=64)
+        h_codes = sb.tile([P, P], U32, align_bytes=64)
+        h_scales = sb.tile([P, P], U8, align_bytes=64)
+        gates = sb.tile([P, GATE_TILES, P], F32)
+
+        def quantise_weights(m):
+            nc.vector.quantize_mx(
+                out=w_codes[:, m, :].bitcast(FP8X4), scales=w_scales[:, m, :], in_=w_grouped[:, m, :]
+            )
+
+        def gate(m):
+            gate_ps = ps_gate.tile([P, P], F32, tag="gate_ps", name="gate_ps")
+            nc.tensor.matmul_mx(
+                out=gate_ps[:],
+                lhsT=w_codes[:, m, :].bitcast(FP8X4),
+                lhsT_scale=w_scales[:, m, :],
+                rhs=h_codes[:].bitcast(FP8X4),
+                rhs_scale=h_scales[:],
+                start=True,
+                stop=True,
+            )
+            nc.scalar.activation(
+                out=gates[:, m, :],
+                in_=gate_ps[:],
+                func=ACT.Tanh if m >= U0 else ACT.Sigmoid,
+                bias=bias_col[:, m : m + 1],
+                scale=1.0,
+            )
+
+        for m in range(F_TILES):
+            nc.vector.tensor_copy(
+                out=w_grouped[:, m, :].rearrange("p (c i t) -> p c t i", i=4, t=PACK),
+                in_=uf_rows[:, :, m * P : (m + 1) * P].rearrange("p t (c i) -> p c t i", i=4),
+            )
+            quantise_weights(m)
+
+        cT = ps_keep.tile([P, F_TILES, P], BF16)
+        for m in range(F_TILES):
+            nc.tensor.transpose(cT[:, m, :], c_rows[:, m * P : (m + 1) * P], ident_bf16[:])
+
+        hT = transpose_words(nc, ps_in, h_rows[:], ident_f32)
+        nc.scalar.copy(
+            out=h_grouped[:].bitcast(F32).rearrange("p (n u) -> p n u", u=2),
+            in_=hT[:].rearrange("p u n -> p n u"),
+        )
+        nc.vector.quantize_mx(out=h_codes[:].bitcast(FP8X4), scales=h_scales[:], in_=h_grouped[:])
+
+        for m in range(F_TILES):
+            gate(m)
+        fc = sb.tile([P, F_TILES, P], F32)
+        nc.vector.tensor_mul(out=fc[:], in0=gates[:, F0:I0, :], in1=cT[:])
+        c_red = sb.tile([P, HALVES, P], F32)
+        nc.vector.tensor_add(out=c_red[:], in0=fc[:, 0:HALVES, :], in1=fc[:, HALVES:F_TILES, :])
+
+        for m in IOU_ORDER:
+            wT = transpose_words(nc, ps_in, ui_rows[:, m - I0, :], ident_f32)
+            nc.scalar.copy(
+                out=w_grouped[:, m, :].bitcast(F32).rearrange("p (r u) -> p r u", u=2),
+                in_=wT[:].rearrange("p u r -> p r u"),
+            )
+            quantise_weights(m)
+            gate(m)
+
+        iu = sb.tile([P, HALVES, P], F32)
+        nc.vector.tensor_mul(out=iu[:], in0=gates[:, I0:O0, :], in1=gates[:, U0:GATE_TILES, :])
+        c_new = sb.tile([P, HALVES, P], F32)
+        nc.vector.tensor_add(out=c_new[:], in0=iu[:], in1=c_red[:])
+        tanh_c = sb.tile([P, HALVES, P], F32)
+        nc.scalar.activation(out=tanh_c[:], in_=c_new[:], func=ACT.Tanh)
+        h_new = sb.tile([P, HALVES, P], F32)
+        nc.vector.tensor_mul(out=h_new[:], in0=gates[:, O0:U0, :], in1=tanh_c[:])
+
+        c_back = ps_keep.tile([P, HALVES, P], F32)
+        for a in range(HALVES):
+            nc.tensor.transpose(c_back[:, a, :], c_new[:, a, :], ident_f32[:])
+        c_out = sb.tile([P, H], F32)
+        nc.vector.tensor_copy(out=c_out[:], in_=c_back[:].rearrange("n a j -> n (a j)"))
+        nc.sync.dma_start(out=out_1, in_=c_out[:])
+
+        h_back = ps_keep.tile([P, HALVES, P], F32)
+        for a in range(HALVES):
+            nc.tensor.transpose(h_back[:, a, :], h_new[:, a, :], ident_f32[:])
+        h_out = sb.tile([P, H], F32)
+        nc.scalar.copy(out=h_out[:], in_=h_back[:].rearrange("n a j -> n (a j)"))
+        nc.sync.dma_start(out=out_0, in_=h_out[:])

@@ -22,7 +22,8 @@ O0 = 6
 U0 = 8
 F_TILES = 4
 GATE_TILES = 10
-IOU_ORDER = (I0, U0, I0 + 1, U0 + 1, O0, O0 + 1)
+IU_TILES = (I0, U0, I0 + 1, U0 + 1)
+O_TILES = (O0, O0 + 1)
 
 FLOPS = 2 * P * K * GATE_TILES * P
 BYTES = 2 * (2 * P * K + K * K + K + 3 * H * K + 3 * H) + 4 * 2 * P * H
@@ -41,8 +42,27 @@ def tile_treelstmcell_s_kernel(tc, h_mail, c_mail, U_f_w, U_f_b, U_iou_w, b_iou,
     with ExitStack() as ctx:
         sb = ctx.enter_context(tc.tile_pool(name="sb", bufs=1))
         ps_in = ctx.enter_context(tc.psum_pool(name="ps_in", bufs=2))
-        ps_gate = ctx.enter_context(tc.psum_pool(name="ps_gate", bufs=3))
         ps_keep = ctx.enter_context(tc.psum_pool(name="ps_keep", bufs=1))
+        ctx.enter_context(tc.manual_schedule())
+
+        bias_rows = sb.tile([P, P], BF16)
+        nc.vector.memset(bias_rows[:], 0.0)
+        nc.scalar.dma_start(out=bias_rows[F0:I0, :], in_=U_f_b[0:K].rearrange("(a p) -> a p", p=P))
+        nc.scalar.dma_start(out=bias_rows[I0:GATE_TILES, :], in_=b_iou.rearrange("o (a p) -> (o a) p", p=P))
+
+        h_rows = sb.tile([P, K], BF16)
+        nc.sync.dma_start(out=h_rows[:], in_=h_mail.rearrange("n k h -> n (k h)"))
+        c_rows = sb.tile([P, K], BF16)
+        nc.sync.dma_start(out=c_rows[:], in_=c_mail.rearrange("n k h -> n (k h)"))
+        uf_rows = sb.tile([P, PACK, K], BF16)
+        for u in range(2):
+            nc.sync.dma_start(
+                out=uf_rows[:, 2 * u : 2 * u + 2, :],
+                in_=U_f_w[2 * P * u : 2 * P * (u + 1), 0:K].rearrange("(p e) c -> p e c", e=2),
+            )
+        ui_rows = sb.tile([P, GATE_TILES - I0, K], BF16)
+        for m in IU_TILES + O_TILES:
+            nc.sync.dma_start(out=ui_rows[:, m - I0, :], in_=U_iou_w[(m - I0) * P : (m - I0 + 1) * P, 0:K])
 
         ident_f32 = sb.tile([P, P], F32)
         make_identity(nc, ident_f32[:])
@@ -53,30 +73,6 @@ def tile_treelstmcell_s_kernel(tc, h_mail, c_mail, U_f_w, U_f_b, U_iou_w, b_iou,
         nc.vector.memset(warm_in[:], 0.0)
         nc.scalar.activation(out=warm_out[:], in_=warm_in[:], func=ACT.Sigmoid)
 
-        bias_rows = sb.tile([P, P], BF16)
-        nc.vector.memset(bias_rows[:], 0.0)
-        nc.scalar.dma_start(out=bias_rows[F0:I0, :], in_=U_f_b[0:K].rearrange("(a p) -> a p", p=P))
-        nc.scalar.dma_start(out=bias_rows[I0:GATE_TILES, :], in_=b_iou.rearrange("o (a p) -> (o a) p", p=P))
-
-        uf_rows = sb.tile([P, PACK, K], BF16)
-        for u in range(2):
-            nc.sync.dma_start(
-                out=uf_rows[:, 2 * u : 2 * u + 2, :],
-                in_=U_f_w[2 * P * u : 2 * P * (u + 1), 0:K].rearrange("(p e) c -> p e c", e=2),
-            )
-        c_rows = sb.tile([P, K], BF16)
-        nc.sync.dma_start(out=c_rows[:], in_=c_mail.rearrange("n k h -> n (k h)"))
-        h_rows = sb.tile([P, K], BF16)
-        nc.sync.dma_start(out=h_rows[:], in_=h_mail.rearrange("n k h -> n (k h)"))
-        ui_rows = sb.tile([P, GATE_TILES - I0, K], BF16)
-        for m in IOU_ORDER:
-            nc.sync.dma_start(out=ui_rows[:, m - I0, :], in_=U_iou_w[(m - I0) * P : (m - I0 + 1) * P, 0:K])
-
-        biasT = ps_in.tile([P, P], BF16, tag="wordsT")
-        nc.tensor.transpose(biasT[:], bias_rows[:], ident_bf16[:])
-        bias_col = sb.tile([P, GATE_TILES], F32)
-        nc.vector.tensor_copy(out=bias_col[:], in_=biasT[:, 0:GATE_TILES])
-
         w_grouped = sb.tile([P, GATE_TILES, P * PACK], BF16, align_bytes=64)
         w_codes = sb.tile([P, GATE_TILES, P], U32, align_bytes=64)
         w_scales = sb.tile([P, GATE_TILES, P], U8, align_bytes=64)
@@ -85,40 +81,43 @@ def tile_treelstmcell_s_kernel(tc, h_mail, c_mail, U_f_w, U_f_b, U_iou_w, b_iou,
         h_scales = sb.tile([P, P], U8, align_bytes=64)
         gates = sb.tile([P, GATE_TILES, P], F32)
 
+        def regroup_f(m):
+            nc.vector.tensor_copy(
+                out=w_grouped[:, m, :].rearrange("p (c i t) -> p c t i", i=4, t=PACK),
+                in_=uf_rows[:, :, m * P : (m + 1) * P].rearrange("p t (c i) -> p c t i", i=4),
+            )
+
+        def transpose_iou(m):
+            wT = transpose_words(nc, ps_in, ui_rows[:, m - I0, :], ident_f32)
+            nc.scalar.copy(
+                out=w_grouped[:, m, :].bitcast(F32).rearrange("p (r u) -> p r u", u=2),
+                in_=wT[:].rearrange("p u r -> p r u"),
+            )
+
         def quantise_weights(m):
             nc.vector.quantize_mx(
                 out=w_codes[:, m, :].bitcast(FP8X4), scales=w_scales[:, m, :], in_=w_grouped[:, m, :]
             )
 
-        def gate(m):
-            gate_ps = ps_gate.tile([P, P], F32, tag="gate_ps", name="gate_ps")
-            nc.tensor.matmul_mx(
-                out=gate_ps[:],
-                lhsT=w_codes[:, m, :].bitcast(FP8X4),
-                lhsT_scale=w_scales[:, m, :],
-                rhs=h_codes[:].bitcast(FP8X4),
-                rhs_scale=h_scales[:],
-                start=True,
-                stop=True,
-            )
-            nc.scalar.activation(
-                out=gates[:, m, :],
-                in_=gate_ps[:],
-                func=ACT.Tanh if m >= U0 else ACT.Sigmoid,
-                bias=bias_col[:, m : m + 1],
-                scale=1.0,
-            )
-
-        for m in range(F_TILES):
-            nc.vector.tensor_copy(
-                out=w_grouped[:, m, :].rearrange("p (c i t) -> p c t i", i=4, t=PACK),
-                in_=uf_rows[:, :, m * P : (m + 1) * P].rearrange("p t (c i) -> p c t i", i=4),
-            )
-            quantise_weights(m)
-
-        cT = ps_keep.tile([P, F_TILES, P], BF16)
-        for m in range(F_TILES):
-            nc.tensor.transpose(cT[:, m, :], c_rows[:, m * P : (m + 1) * P], ident_bf16[:])
+        def gate_group(tiles, bank):
+            for s, m in enumerate(tiles):
+                nc.tensor.matmul_mx(
+                    out=bank[:, s, :],
+                    lhsT=w_codes[:, m, :].bitcast(FP8X4),
+                    lhsT_scale=w_scales[:, m, :],
+                    rhs=h_codes[:].bitcast(FP8X4),
+                    rhs_scale=h_scales[:],
+                    start=True,
+                    stop=True,
+                )
+            for s, m in enumerate(tiles):
+                nc.scalar.activation(
+                    out=gates[:, m, :],
+                    in_=bank[:, s, :],
+                    func=ACT.Tanh if m >= U0 else ACT.Sigmoid,
+                    bias=bias_col[:, m : m + 1],
+                    scale=1.0,
+                )
 
         hT = transpose_words(nc, ps_in, h_rows[:], ident_f32)
         nc.scalar.copy(
@@ -127,41 +126,56 @@ def tile_treelstmcell_s_kernel(tc, h_mail, c_mail, U_f_w, U_f_b, U_iou_w, b_iou,
         )
         nc.vector.quantize_mx(out=h_codes[:].bitcast(FP8X4), scales=h_scales[:], in_=h_grouped[:])
 
+        biasT = ps_in.tile([P, P], BF16, tag="wordsT")
+        nc.tensor.transpose(biasT[:], bias_rows[:], ident_bf16[:])
+        bias_col = sb.tile([P, GATE_TILES], F32)
+        nc.vector.tensor_copy(out=bias_col[:], in_=biasT[:, 0:GATE_TILES])
+
+        cT = ps_keep.tile([P, F_TILES, P], BF16)
         for m in range(F_TILES):
-            gate(m)
+            nc.tensor.transpose(cT[:, m, :], c_rows[:, m * P : (m + 1) * P], ident_bf16[:])
+
+        regroup_f(0)
+        for m in range(1, F_TILES):
+            regroup_f(m)
+            quantise_weights(m - 1)
+        quantise_weights(F_TILES - 1)
+
+        for m in IU_TILES:
+            transpose_iou(m)
+            quantise_weights(m)
+        f_bank = ps_keep.tile([P, F_TILES, P], F32)
+        gate_group(range(F_TILES), f_bank)
+        for m in O_TILES:
+            transpose_iou(m)
         fc = sb.tile([P, F_TILES, P], F32)
         nc.vector.tensor_mul(out=fc[:], in0=gates[:, F0:I0, :], in1=cT[:])
+        for m in O_TILES:
+            quantise_weights(m)
+        iu_bank = ps_keep.tile([P, len(IU_TILES), P], F32)
+        gate_group(IU_TILES, iu_bank)
         c_red = sb.tile([P, HALVES, P], F32)
         nc.vector.tensor_add(out=c_red[:], in0=fc[:, 0:HALVES, :], in1=fc[:, HALVES:F_TILES, :])
-
-        for m in IOU_ORDER:
-            wT = transpose_words(nc, ps_in, ui_rows[:, m - I0, :], ident_f32)
-            nc.scalar.copy(
-                out=w_grouped[:, m, :].bitcast(F32).rearrange("p (r u) -> p r u", u=2),
-                in_=wT[:].rearrange("p u r -> p r u"),
-            )
-            quantise_weights(m)
-            gate(m)
+        o_bank = ps_keep.tile([P, len(O_TILES), P], F32)
+        gate_group(O_TILES, o_bank)
 
         iu = sb.tile([P, HALVES, P], F32)
         nc.vector.tensor_mul(out=iu[:], in0=gates[:, I0:O0, :], in1=gates[:, U0:GATE_TILES, :])
         c_new = sb.tile([P, HALVES, P], F32)
         nc.vector.tensor_add(out=c_new[:], in0=iu[:], in1=c_red[:])
-        tanh_c = sb.tile([P, HALVES, P], F32)
-        nc.scalar.activation(out=tanh_c[:], in_=c_new[:], func=ACT.Tanh)
-        h_new = sb.tile([P, HALVES, P], F32)
-        nc.vector.tensor_mul(out=h_new[:], in0=gates[:, O0:U0, :], in1=tanh_c[:])
 
-        c_back = ps_keep.tile([P, HALVES, P], F32)
+        c_back = ps_keep.tile([P, H], F32)
         for a in range(HALVES):
-            nc.tensor.transpose(c_back[:, a, :], c_new[:, a, :], ident_f32[:])
+            nc.tensor.transpose(c_back[:, a * P : (a + 1) * P], c_new[:, a, :], ident_f32[:])
+        tanh_c = sb.tile([P, H], F32)
+        nc.scalar.activation(out=tanh_c[:], in_=c_back[:], func=ACT.Tanh)
         c_out = sb.tile([P, H], F32)
-        nc.vector.tensor_copy(out=c_out[:], in_=c_back[:].rearrange("n a j -> n (a j)"))
+        nc.vector.tensor_copy(out=c_out[:], in_=c_back[:])
         nc.sync.dma_start(out=out_1, in_=c_out[:])
 
-        h_back = ps_keep.tile([P, HALVES, P], F32)
+        o_back = ps_keep.tile([P, H], F32)
         for a in range(HALVES):
-            nc.tensor.transpose(h_back[:, a, :], h_new[:, a, :], ident_f32[:])
+            nc.tensor.transpose(o_back[:, a * P : (a + 1) * P], gates[:, O0 + a, :], ident_f32[:])
         h_out = sb.tile([P, H], F32)
-        nc.scalar.copy(out=h_out[:], in_=h_back[:].rearrange("n a j -> n (a j)"))
+        nc.vector.tensor_mul(out=h_out[:], in0=tanh_c[:], in1=o_back[:])
         nc.sync.dma_start(out=out_0, in_=h_out[:])

@@ -43,6 +43,7 @@ def tile_treelstmcell_s_kernel(tc, h_mail, c_mail, U_f_w, U_f_b, U_iou_w, b_iou,
         sb = ctx.enter_context(tc.tile_pool(name="sb", bufs=1))
         ps_in = ctx.enter_context(tc.psum_pool(name="ps_in", bufs=2))
         ps_keep = ctx.enter_context(tc.psum_pool(name="ps_keep", bufs=1))
+        ps_bank = ctx.enter_context(tc.psum_pool(name="ps_bank", bufs=5))
         ctx.enter_context(tc.manual_schedule())
 
         bias_rows = sb.tile([P, P], BF16)
@@ -144,38 +145,50 @@ def tile_treelstmcell_s_kernel(tc, h_mail, c_mail, U_f_w, U_f_b, U_iou_w, b_iou,
         for m in IU_TILES:
             transpose_iou(m)
             quantise_weights(m)
-        f_bank = ps_keep.tile([P, F_TILES, P], F32)
+        f_bank = ps_bank.tile([P, F_TILES, P], F32, tag="bank")
         gate_group(range(F_TILES), f_bank)
         for m in O_TILES:
             transpose_iou(m)
         fc = sb.tile([P, F_TILES, P], F32)
-        nc.vector.tensor_mul(out=fc[:], in0=gates[:, F0:I0, :], in1=cT[:])
+        for a in range(HALVES):
+            nc.vector.tensor_mul(
+                out=fc[:, a:F_TILES:HALVES, :], in0=gates[:, a:F_TILES:HALVES, :], in1=cT[:, a:F_TILES:HALVES, :]
+            )
         for m in O_TILES:
             quantise_weights(m)
-        iu_bank = ps_keep.tile([P, len(IU_TILES), P], F32)
+        iu_bank = ps_bank.tile([P, len(IU_TILES), P], F32, tag="bank")
         gate_group(IU_TILES, iu_bank)
         c_red = sb.tile([P, HALVES, P], F32)
-        nc.vector.tensor_add(out=c_red[:], in0=fc[:, 0:HALVES, :], in1=fc[:, HALVES:F_TILES, :])
-        o_bank = ps_keep.tile([P, len(O_TILES), P], F32)
+        for a in range(HALVES):
+            nc.vector.tensor_add(out=c_red[:, a, :], in0=fc[:, a, :], in1=fc[:, HALVES + a, :])
+        o_bank = ps_bank.tile([P, len(O_TILES), P], F32, tag="bank")
         gate_group(O_TILES, o_bank)
 
         iu = sb.tile([P, HALVES, P], F32)
-        nc.vector.tensor_mul(out=iu[:], in0=gates[:, I0:O0, :], in1=gates[:, U0:GATE_TILES, :])
-        c_new = sb.tile([P, HALVES, P], F32)
-        nc.vector.tensor_add(out=c_new[:], in0=iu[:], in1=c_red[:])
-
-        c_back = ps_keep.tile([P, H], F32)
         for a in range(HALVES):
-            nc.tensor.transpose(c_back[:, a * P : (a + 1) * P], c_new[:, a, :], ident_f32[:])
+            nc.vector.tensor_mul(out=iu[:, a, :], in0=gates[:, I0 + a, :], in1=gates[:, U0 + a, :])
+        c_new = sb.tile([P, HALVES, P], F32)
+        for a in range(HALVES):
+            nc.vector.tensor_add(out=c_new[:, a, :], in0=iu[:, a, :], in1=c_red[:, a, :])
+
+        o_back = ps_bank.tile([P, H], F32, tag="bank")
+        nc.tensor.transpose(o_back[:, 0:P], gates[:, O0, :], ident_f32[:])
+        c_back = []
+        for a in range(HALVES):
+            c_back.append(ps_bank.tile([P, P], F32, tag="bank", name="c_back"))
+            nc.tensor.transpose(c_back[a][:], c_new[:, a, :], ident_f32[:])
+        nc.tensor.transpose(o_back[:, P:H], gates[:, O0 + 1, :], ident_f32[:])
+
         tanh_c = sb.tile([P, H], F32)
-        nc.scalar.activation(out=tanh_c[:], in_=c_back[:], func=ACT.Tanh)
+        for a in range(HALVES):
+            nc.scalar.activation(out=tanh_c[:, a * P : (a + 1) * P], in_=c_back[a][:], func=ACT.Tanh)
         c_out = sb.tile([P, H], F32)
-        nc.vector.tensor_copy(out=c_out[:], in_=c_back[:])
+        for a in range(HALVES):
+            nc.scalar.copy(out=c_out[:, a * P : (a + 1) * P], in_=c_back[a][:])
         nc.sync.dma_start(out=out_1, in_=c_out[:])
 
-        o_back = ps_keep.tile([P, H], F32)
-        for a in range(HALVES):
-            nc.tensor.transpose(o_back[:, a * P : (a + 1) * P], gates[:, O0 + a, :], ident_f32[:])
         h_out = sb.tile([P, H], F32)
-        nc.vector.tensor_mul(out=h_out[:], in0=tanh_c[:], in1=o_back[:])
+        for a in range(HALVES):
+            half = slice(a * P, (a + 1) * P)
+            nc.vector.tensor_mul(out=h_out[:, half], in0=tanh_c[:, half], in1=o_back[:, half])
         nc.sync.dma_start(out=out_0, in_=h_out[:])

@@ -44,7 +44,6 @@ def tile_treelstmcell_s_kernel(tc, h_mail, c_mail, U_f_w, U_f_b, U_iou_w, b_iou,
         ps_in = ctx.enter_context(tc.psum_pool(name="ps_in", bufs=2))
         ps_keep = ctx.enter_context(tc.psum_pool(name="ps_keep", bufs=1))
         ps_bank = ctx.enter_context(tc.psum_pool(name="ps_bank", bufs=5))
-        ctx.enter_context(tc.manual_schedule())
 
         bias_rows = sb.tile([P, P], BF16)
         nc.vector.memset(bias_rows[:], 0.0)

@@ -44,6 +44,7 @@ def tile_treelstmcell_s_kernel(tc, h_mail, c_mail, U_f_w, U_f_b, U_iou_w, b_iou,
         ps_in = ctx.enter_context(tc.psum_pool(name="ps_in", bufs=2))
         ps_keep = ctx.enter_context(tc.psum_pool(name="ps_keep", bufs=1))
         ps_bank = ctx.enter_context(tc.psum_pool(name="ps_bank", bufs=5))
+        ctx.enter_context(tc.manual_schedule())
 
         bias_rows = sb.tile([P, P], BF16)
         nc.vector.memset(bias_rows[:], 0.0)
@@ -166,17 +167,19 @@ def tile_treelstmcell_s_kernel(tc, h_mail, c_mail, U_f_w, U_f_b, U_iou_w, b_iou,
         iu = sb.tile([P, HALVES, P], F32)
         for a in range(HALVES):
             nc.vector.tensor_mul(out=iu[:, a, :], in0=gates[:, I0 + a, :], in1=gates[:, U0 + a, :])
-        c_new = sb.tile([P, HALVES, P], F32)
-        for a in range(HALVES):
-            nc.vector.tensor_add(out=c_new[:, a, :], in0=iu[:, a, :], in1=c_red[:, a, :])
 
-        o_back = ps_bank.tile([P, H], F32, tag="bank")
-        nc.tensor.transpose(o_back[:, 0:P], gates[:, O0, :], ident_f32[:])
         c_back = []
         for a in range(HALVES):
             c_back.append(ps_bank.tile([P, P], F32, tag="bank", name="c_back"))
-            nc.tensor.transpose(c_back[a][:], c_new[:, a, :], ident_f32[:])
-        nc.tensor.transpose(o_back[:, P:H], gates[:, O0 + 1, :], ident_f32[:])
+            nc.tensor.matmul(
+                out=c_back[a][:], lhsT=c_red[:, a, :], rhs=ident_f32[:], is_transpose=True, start=True, stop=False
+            )
+        o_back = ps_bank.tile([P, H], F32, tag="bank")
+        for a in range(HALVES):
+            nc.tensor.matmul(
+                out=c_back[a][:], lhsT=iu[:, a, :], rhs=ident_f32[:], is_transpose=True, start=False, stop=True
+            )
+            nc.tensor.transpose(o_back[:, a * P : (a + 1) * P], gates[:, O0 + a, :], ident_f32[:])
 
         tanh_c = sb.tile([P, H], F32)
         for a in range(HALVES):

from contextlib import ExitStack

import concourse.mybir as mybir
from concourse.masks import make_identity

F32 = mybir.dt.float32
BF16 = mybir.dt.bfloat16
U32 = mybir.dt.uint32
U8 = mybir.dt.uint8
FP8X4 = mybir.dt.float8_e4m3fn_x4
ACT = mybir.ActivationFunctionType

P = 128
PACK = 4
K = P * PACK
H = 256
HALVES = H // P

F0 = 0
I0 = 4
O0 = 6
U0 = 8
F_TILES = 4
GATE_TILES = 10
IU_TILES = (I0, U0, I0 + 1, U0 + 1)
O_TILES = (O0, O0 + 1)

FLOPS = 2 * P * K * GATE_TILES * P
BYTES = 2 * (2 * P * K + K * K + K + 3 * H * K + 3 * H) + 4 * 2 * P * H


def transpose_words(nc, psum, rows, ident_f32):
    words = rows.bitcast(F32)
    wordsT = psum.tile([P, 2, P], F32, tag="wordsT", name="wordsT")
    for u in range(2):
        nc.tensor.transpose(wordsT[:, u, :], words[:, u * P : (u + 1) * P], ident_f32[:])
    return wordsT


def tile_treelstmcell_s_kernel(tc, h_mail, c_mail, U_f_w, U_f_b, U_iou_w, b_iou, out_0, out_1):
    nc = tc.nc
    with ExitStack() as ctx:
        sb = ctx.enter_context(tc.tile_pool(name="sb", bufs=1))
        ps_in = ctx.enter_context(tc.psum_pool(name="ps_in", bufs=2))
        ps_keep = ctx.enter_context(tc.psum_pool(name="ps_keep", bufs=1))
        ps_bank = ctx.enter_context(tc.psum_pool(name="ps_bank", bufs=5))
        ctx.enter_context(tc.manual_schedule())

        bias_rows = sb.tile([P, P], BF16)
        nc.vector.memset(bias_rows[:], 0.0)
        nc.scalar.dma_start(out=bias_rows[F0:I0, :], in_=U_f_b[0:K].rearrange("(a p) -> a p", p=P))
        nc.scalar.dma_start(out=bias_rows[I0:GATE_TILES, :], in_=b_iou.rearrange("o (a p) -> (o a) p", p=P))

        h_rows = sb.tile([P, K], BF16)
        nc.sync.dma_start(out=h_rows[:], in_=h_mail.rearrange("n k h -> n (k h)"))
        c_rows = sb.tile([P, K], BF16)
        nc.sync.dma_start(out=c_rows[:], in_=c_mail.rearrange("n k h -> n (k h)"))
        uf_rows = sb.tile([P, PACK, K], BF16)
        for u in range(2):
            nc.sync.dma_start(
                out=uf_rows[:, 2 * u : 2 * u + 2, :],
                in_=U_f_w[2 * P * u : 2 * P * (u + 1), 0:K].rearrange("(p e) c -> p e c", e=2),
            )
        ui_rows = sb.tile([P, GATE_TILES - I0, K], BF16)
        for m in IU_TILES + O_TILES:
            nc.sync.dma_start(out=ui_rows[:, m - I0, :], in_=U_iou_w[(m - I0) * P : (m - I0 + 1) * P, 0:K])

        ident_f32 = sb.tile([P, P], F32)
        make_identity(nc, ident_f32[:])
        ident_bf16 = sb.tile([P, P], BF16)
        make_identity(nc, ident_bf16[:])
        warm_in = sb.tile([P, 1], F32)
        warm_out = sb.tile([P, 1], F32)
        nc.vector.memset(warm_in[:], 0.0)
        nc.scalar.activation(out=warm_out[:], in_=warm_in[:], func=ACT.Sigmoid)

        w_grouped = sb.tile([P, GATE_TILES, P * PACK], BF16, align_bytes=64)
        w_codes = sb.tile([P, GATE_TILES, P], U32, align_bytes=64)
        w_scales = sb.tile([P, GATE_TILES, P], U8, align_bytes=64)
        h_grouped = sb.tile([P, P * PACK], BF16, align_bytes=64)
        h_codes = sb.tile([P, P], U32, align_bytes=64)
        h_scales = sb.tile([P, P], U8, align_bytes=64)
        gates = sb.tile([P, GATE_TILES, P], F32)

        def regroup_f(m):
            nc.vector.tensor_copy(
                out=w_grouped[:, m, :].rearrange("p (c i t) -> p c t i", i=4, t=PACK),
                in_=uf_rows[:, :, m * P : (m + 1) * P].rearrange("p t (c i) -> p c t i", i=4),
            )

        def transpose_iou(m):
            wT = transpose_words(nc, ps_in, ui_rows[:, m - I0, :], ident_f32)
            nc.scalar.copy(
                out=w_grouped[:, m, :].bitcast(F32).rearrange("p (r u) -> p r u", u=2),
                in_=wT[:].rearrange("p u r -> p r u"),
            )

        def quantise_weights(m):
            nc.vector.quantize_mx(
                out=w_codes[:, m, :].bitcast(FP8X4), scales=w_scales[:, m, :], in_=w_grouped[:, m, :]
            )

        def gate_group(tiles, bank):
            for s, m in enumerate(tiles):
                nc.tensor.matmul_mx(
                    out=bank[:, s, :],
                    lhsT=w_codes[:, m, :].bitcast(FP8X4),
                    lhsT_scale=w_scales[:, m, :],
                    rhs=h_codes[:].bitcast(FP8X4),
                    rhs_scale=h_scales[:],
                    start=True,
                    stop=True,
                )
            for s, m in enumerate(tiles):
                nc.scalar.activation(
                    out=gates[:, m, :],
                    in_=bank[:, s, :],
                    func=ACT.Tanh if m >= U0 else ACT.Sigmoid,
                    bias=bias_col[:, m : m + 1],
                    scale=1.0,
                )

        hT = transpose_words(nc, ps_in, h_rows[:], ident_f32)
        nc.scalar.copy(
            out=h_grouped[:].bitcast(F32).rearrange("p (n u) -> p n u", u=2),
            in_=hT[:].rearrange("p u n -> p n u"),
        )
        nc.vector.quantize_mx(out=h_codes[:].bitcast(FP8X4), scales=h_scales[:], in_=h_grouped[:])

        biasT = ps_in.tile([P, P], BF16, tag="wordsT")
        nc.tensor.transpose(biasT[:], bias_rows[:], ident_bf16[:])
        bias_col = sb.tile([P, GATE_TILES], F32)
        nc.vector.tensor_copy(out=bias_col[:], in_=biasT[:, 0:GATE_TILES])

        cT = ps_keep.tile([P, F_TILES, P], BF16)
        for m in range(F_TILES):
            nc.tensor.transpose(cT[:, m, :], c_rows[:, m * P : (m + 1) * P], ident_bf16[:])

        regroup_f(0)
        for m in range(1, F_TILES):
            regroup_f(m)
            quantise_weights(m - 1)
        quantise_weights(F_TILES - 1)

        for m in IU_TILES:
            transpose_iou(m)
            quantise_weights(m)
        f_bank = ps_bank.tile([P, F_TILES, P], F32, tag="bank")
        gate_group(range(F_TILES), f_bank)
        for m in O_TILES:
            transpose_iou(m)
        fc = sb.tile([P, F_TILES, P], F32)
        for a in range(HALVES):
            nc.vector.tensor_mul(
                out=fc[:, a:F_TILES:HALVES, :], in0=gates[:, a:F_TILES:HALVES, :], in1=cT[:, a:F_TILES:HALVES, :]
            )
        for m in O_TILES:
            quantise_weights(m)
        iu_bank = ps_bank.tile([P, len(IU_TILES), P], F32, tag="bank")
        gate_group(IU_TILES, iu_bank)
        c_red = sb.tile([P, HALVES, P], F32)
        for a in range(HALVES):
            nc.vector.tensor_add(out=c_red[:, a, :], in0=fc[:, a, :], in1=fc[:, HALVES + a, :])
        o_bank = ps_bank.tile([P, len(O_TILES), P], F32, tag="bank")
        gate_group(O_TILES, o_bank)

        iu = sb.tile([P, HALVES, P], F32)
        for a in range(HALVES):
            nc.vector.tensor_mul(out=iu[:, a, :], in0=gates[:, I0 + a, :], in1=gates[:, U0 + a, :])

        c_back = []
        for a in range(HALVES):
            c_back.append(ps_bank.tile([P, P], F32, tag="bank", name="c_back"))
            nc.tensor.matmul(
                out=c_back[a][:], lhsT=c_red[:, a, :], rhs=ident_f32[:], is_transpose=True, start=True, stop=False
            )
        o_back = ps_bank.tile([P, H], F32, tag="bank")
        for a in range(HALVES):
            nc.tensor.matmul(
                out=c_back[a][:], lhsT=iu[:, a, :], rhs=ident_f32[:], is_transpose=True, start=False, stop=True
            )
            nc.tensor.transpose(o_back[:, a * P : (a + 1) * P], gates[:, O0 + a, :], ident_f32[:])

        tanh_c = sb.tile([P, H], F32)
        for a in range(HALVES):
            nc.scalar.activation(out=tanh_c[:, a * P : (a + 1) * P], in_=c_back[a][:], func=ACT.Tanh)
        c_out = sb.tile([P, H], F32)
        for a in range(HALVES):
            nc.scalar.copy(out=c_out[:, a * P : (a + 1) * P], in_=c_back[a][:])
        nc.sync.dma_start(out=out_1, in_=c_out[:])

        h_out = sb.tile([P, H], F32)
        for a in range(HALVES):
            half = slice(a * P, (a + 1) * P)
            nc.vector.tensor_mul(out=h_out[:, half], in0=tanh_c[:, half], in1=o_back[:, half])
        nc.sync.dma_start(out=out_0, in_=h_out[:])
